import numpy as np
import ml_dtypes


def mxq(x, axis, fmt="e4m3"):
    dtype, down = {"e4m3": (ml_dtypes.float8_e4m3fn, 7), "e5m2": (ml_dtypes.float8_e5m2, 14)}[fmt]
    v = np.moveaxis(np.asarray(x, np.float32).astype(ml_dtypes.bfloat16).astype(np.float64), axis, -1)
    blocks = v.reshape(v.shape[:-1] + (-1, 32))
    amax = np.abs(blocks).max(-1, keepdims=True)
    byte = np.maximum(np.where(amax > 0, np.frexp(amax)[1] - 1 + 127, 0) - down, 1)
    scale = np.exp2(byte - 127.0)
    codes = (blocks / scale).astype(np.float32).astype(dtype).astype(np.float64)
    return np.moveaxis((codes * scale).reshape(v.shape), -1, axis)


WIDE = False


def mx_kscale(k):
    if not WIDE:
        return np.ones(k)
    levels = np.array([10, -10, 5, -5, 0])
    if k % 512:
        return np.exp2(np.random.permutation(np.resize(levels, k // 32))).repeat(32)
    a = np.empty((k // 512, 16))
    for p in range(k // 512):
        a[p, :8] = np.random.permutation(np.resize(levels, 8))
        for g in range(8):
            far = levels[np.abs(levels - a[p, g]) >= 10]
            a[p, g + 8] = far[np.random.randint(len(far))]
    return np.exp2(a.ravel()).repeat(32)


BF16 = ml_dtypes.bfloat16


def bf(x):
    return np.asarray(x, np.float32).astype(BF16)


def f64(x):
    return np.asarray(x).astype(np.float64)


B, N, F, O, E, K = 16, 512, 512, 16, 16, 3


def setup_inputs():
    s = mx_kscale(F)
    return {"x_g": bf(np.random.standard_normal((B, K, N, F)) * s),
            "emb": bf(np.random.standard_normal((B, N, E))),
            "weights_pool": bf(np.random.standard_normal((E, K, F, O)) * 0.5 / np.sqrt(K * F) / s[:, None]),
            "bias_pool": bf(np.random.standard_normal((E, O)) * 0.3)}


def reference(x_g, emb, weights_pool, bias_pool):
    xg, w, g = f64(x_g), f64(weights_pool), f64(emb)
    z = 0.0
    for k in range(K):
        wk = w[:, k].transpose(1, 0, 2).reshape(F, E * O)
        z = z + (mxq(xg[:, k], 2, "e4m3") @ mxq(wk, 0, "e4m3"))
    z = z.reshape(B, N, E, O)
    out = (g[:, :, :, None] * z).sum(2)
    return out + (g[:, :, :, None] * f64(bias_pool)[None, None, :, :]).sum(2)

@@ -1,0 +1,274 @@
+from contextlib import ExitStack
+
+import concourse.mybir as mybir
+from concourse.masks import make_identity
+
+BF16 = mybir.dt.bfloat16
+F32 = mybir.dt.float32
+U32 = mybir.dt.uint32
+U8 = mybir.dt.uint8
+FP8X4 = mybir.dt.float8_e4m3fn_x4
+ADD = mybir.AluOpType.add
+MULT = mybir.AluOpType.mult
+AX = mybir.AxisListType.X
+
+P = 128
+B, KC, N, F, O, E = 16, 3, 512, 512, 16, 16
+NT = N // P
+UNITS = KC * NT
+NB = 6
+BO = NT * O
+GP_LAST = B - 3
+FINE = 3
+
+FLOPS = 2 * B * N * KC * F * E * O + 4 * B * N * E * O
+
+
+def tile_dygcn_pb_t_kernel(tc, x_g, emb, weights_pool, bias_pool, out):
+    nc = tc.nc
+    with ExitStack() as ctx:
+        const = ctx.enter_context(tc.tile_pool(name="const", bufs=1))
+        xpool = ctx.enter_context(tc.tile_pool(name="xpool", bufs=NB))
+        gpool = ctx.enter_context(tc.tile_pool(name="gpool", bufs=3))
+        cpool = ctx.enter_context(tc.tile_pool(name="cpool", bufs=3))
+        ppool = ctx.enter_context(tc.tile_pool(name="ppool", bufs=4))
+        ps_t = ctx.enter_context(tc.psum_pool(name="ps_t", bufs=6))
+        ps_z = ctx.enter_context(tc.psum_pool(name="ps_z", bufs=2))
+        ctx.enter_context(tc.manual_schedule())
+
+        ident_f = const.tile([P, P], F32, name="ident_f")
+        ident_b = const.tile([P, P], BF16, name="ident_b")
+        w_raw = const.tile([P, KC * E * 4 * O], BF16, name="w_raw")
+        w_grp = const.tile([P, KC * 512], F32, name="w_grp", align_bytes=64)
+        w_cod = const.tile([P, KC * 256], U32, name="w_cod", align_bytes=64)
+        w_scl = const.tile([P, KC * 256], U8, name="w_scl", align_bytes=64)
+        g_bf = const.tile([P, B * NT * E], BF16, name="g_bf")
+        g_32 = const.tile([P, B * NT, E], F32, name="g_32")
+        g_t = const.tile([P, B * NT * E], BF16, name="g_t")
+        bdiag = const.tile([P, P], BF16, name="bdiag")
+        gb = const.tile([P, B * BO], F32, name="gb")
+        o_sb = const.tile([P, B * BO], F32, name="o_sb")
+
+        xs_of = {}
+        gr_of = {}
+        cd_of = {}
+        sc_of = {}
+        zp_of = {}
+        pr_of = {}
+        q1_of = {}
+
+        def load_x(b, split):
+            xs = xpool.tile([P, KC * NT * F], BF16, name="xs")
+            xs_of[b] = xs
+            src = x_g[b].rearrange("k (p t) f -> p k (t f)", t=NT)
+            dst = xs[:].rearrange("p (k c) -> p k c", k=KC)
+            if split:
+                for k in range(KC):
+                    nc.sync.dma_start(out=dst[:, k, :], in_=src[:, k, :])
+            else:
+                nc.sync.dma_start(out=dst, in_=src)
+
+        def new_batch(b):
+            gr_of[b] = gpool.tile([P, UNITS * 256], F32, name="gr", align_bytes=64)
+            cd_of[b] = cpool.tile([P, UNITS * P], U32, name="cd", align_bytes=64)
+            sc_of[b] = cpool.tile([P, UNITS * P], U8, name="sc", align_bytes=64)
+
+        def transpose_bank(b, j):
+            xw = xs_of[b][:].bitcast(F32)
+            tp = ps_t.tile([P, 512], F32, name="tp", tag="tp")
+            for s in range(4):
+                c0 = 256 * (2 * j + s // 2)
+                nc.tensor.transpose(tp[:, P * s : P * s + P], xw[:, c0 + s % 2 : c0 + 256 : 2], ident_f[:])
+            nc.scalar.copy(
+                out=gr_of[b][:, 512 * j : 512 * j + 512].rearrange("p (a n u) -> p a n u", a=2, u=2),
+                in_=tp[:].rearrange("p (a u n) -> p a n u", a=2, u=2),
+            )
+
+        def quantise(b, c0, cw):
+            nc.vector.quantize_mx(
+                out=cd_of[b][:, c0 : c0 + cw].bitcast(FP8X4),
+                scales=sc_of[b][:, c0 : c0 + cw],
+                in_=gr_of[b][:, 2 * c0 : 2 * (c0 + cw)].bitcast(BF16),
+            )
+
+        def mx(b, h):
+            cd = cd_of[b]
+            sc = sc_of[b]
+            zp = ps_z.tile([P, 512], F32, name="zp", tag="zp")
+            zp_of[(b, h)] = zp
+            for a in range(2):
+                for k in range(KC):
+                    c0 = P * (NT * k + 2 * h + a)
+                    nc.tensor.matmul_mx(
+                        out=zp[:, 256 * a : 256 * a + 256],
+                        lhsT=cd[:, c0 : c0 + P].bitcast(FP8X4),
+                        lhsT_scale=sc[:, c0 : c0 + P],
+                        rhs=w_cod[:, 256 * k : 256 * k + 256].bitcast(FP8X4),
+                        rhs_scale=w_scl[:, 256 * k : 256 * k + 256],
+                        start=(k == 0),
+                        stop=(k == KC - 1),
+                    )
+
+        def weigh(b, h):
+            if h == 0:
+                pr_of[b] = ppool.tile([P, NT * O * E], F32, name="pr")
+            t0 = NT * b + 2 * h
+            nc.vector.tensor_tensor(
+                out=pr_of[b][:, 512 * h : 512 * h + 512].rearrange("p (a o e) -> p a o e", a=2, o=O),
+                in0=zp_of[(b, h)][:].rearrange("p (a o e) -> p a o e", a=2, o=O),
+                in1=g_32[:, t0 : t0 + 2, :].unsqueeze(2).to_broadcast([P, 2, O, E]),
+                op=MULT,
+            )
+
+        def fold_16_to_8(b, h):
+            if h == 0 and b % 2 == 0:
+                q1_of[b // 2] = ppool.tile([P, 2 * BO * 8], F32, name="q1")
+            pv = pr_of[b][:, 512 * h : 512 * h + 512].rearrange("p (c e) -> p c e", e=E)
+            c0 = 512 * (b % 2) + 256 * h
+            nc.gpsimd.tensor_tensor(
+                out=q1_of[b // 2][:, c0 : c0 + 256].rearrange("p (c e) -> p c e", e=8),
+                in0=pv[:, :, 0:8],
+                in1=pv[:, :, 8:16],
+                op=ADD,
+            )
+
+        def finish(b0, nb, terms, width, adder):
+            rs = ppool.tile([P, 2 * BO], F32, name="rs")
+            nc.vector.tensor_reduce(
+                out=rs[:, 0 : nb * BO], in_=terms.rearrange("p (c e) -> p c e", e=width), axis=AX, op=ADD
+            )
+            cols = slice(BO * b0, BO * (b0 + nb))
+            adder.tensor_tensor(out=o_sb[:, cols], in0=rs[:, 0 : nb * BO], in1=gb[:, cols], op=ADD)
+            nc.sync.dma_start(
+                out=out[b0 : b0 + nb].rearrange("b (p t) o -> p b (t o)", t=NT),
+                in_=o_sb[:, cols].rearrange("p (b c) -> p b c", b=nb),
+            )
+
+        def finish_on_gpsimd(b0):
+            terms = q1_of[b0 // 2][:]
+            width = 8
+            while width > 1:
+                half = width // 2
+                tv = terms.rearrange("p (c e) -> p c e", e=width)
+                nxt = ppool.tile([P, 2 * BO * half], F32, name="fold%d" % half)
+                nc.gpsimd.tensor_tensor(
+                    out=nxt[:].rearrange("p (c e) -> p c e", e=half),
+                    in0=tv[:, :, 0:half],
+                    in1=tv[:, :, half:width],
+                    op=ADD,
+                )
+                terms = nxt[:]
+                width = half
+            cols = slice(BO * b0, BO * (b0 + 2))
+            nc.gpsimd.tensor_tensor(out=o_sb[:, cols], in0=terms, in1=gb[:, cols], op=ADD)
+            nc.sync.dma_start(
+                out=out[b0 : b0 + 2].rearrange("b (p t) o -> p b (t o)", t=NT),
+                in_=o_sb[:, cols].rearrange("p (b c) -> p b c", b=2),
+            )
+
+        def bias_product_turn():
+            tpb = ps_t.tile([P, 1024], BF16, name="tpb", tag="tp")
+            for c in range(8):
+                nc.tensor.transpose(tpb[:, P * c : P * c + P], g_bf[:, P * c : P * c + P], ident_b[:])
+            nc.scalar.copy(out=g_t[:], in_=tpb[:])
+            nc.vector.tensor_copy(out=g_32[:].rearrange("p t e -> p (t e)"), in_=g_bf[:])
+
+        def bias_product_multiply():
+            for half in range(2):
+                gp = ps_t.tile([P, 512], F32, name="gp", tag="tp")
+                for c4 in range(4):
+                    c = 4 * half + c4
+                    nc.tensor.matmul(
+                        gp[:, P * c4 : P * c4 + P],
+                        lhsT=g_t[:, P * c : P * c + P],
+                        rhs=bdiag[:],
+                        start=True,
+                        stop=True,
+                    )
+                nc.scalar.copy(out=gb[:, 512 * half : 512 * half + 512], in_=gp[:])
+
+        def weigh_and_fold(b, h):
+            weigh(b, h)
+            if b <= GP_LAST:
+                fold_16_to_8(b, h)
+
+        make_identity(nc, ident_f[:])
+        make_identity(nc, ident_b[:])
+        nc.vector.memset(bdiag[:], 0.0)
+        for i in range(8):
+            nc.gpsimd.dma_start(out=bdiag[16 * i : 16 * i + 16, 16 * i : 16 * i + 16], in_=bias_pool)
+
+        load_x(0, True)
+        for k in range(KC):
+            nc.sync.dma_start(
+                out=w_raw[:].rearrange("p (k e c) -> p k e c", k=KC, e=E)[:, k],
+                in_=weights_pool.rearrange("e k (p t) o -> p k e (t o)", t=4)[:, k],
+            )
+        nc.sync.dma_start(
+            out=g_bf[:].rearrange("p (b c) -> p b c", b=B),
+            in_=emb.rearrange("b (p t) e -> p b (t e)", t=NT),
+        )
+        for b in range(1, NB):
+            load_x(b, b <= FINE)
+
+        def w_turn(k, copy):
+            copy(
+                out=w_grp[:, 512 * k : 512 * k + 512].bitcast(BF16).rearrange("p (o e t) -> p o e t", o=O, e=E),
+                in_=w_raw[:, 1024 * k : 1024 * k + 1024].rearrange("p (e t o) -> p o e t", e=E, t=4),
+            )
+
+        new_batch(0)
+        for k in range(KC):
+            transpose_bank(0, 2 * k)
+            transpose_bank(0, 2 * k + 1)
+            quantise(0, 512 * k, 512)
+        w_turn(0, nc.vector.tensor_copy)
+        w_turn(1, nc.scalar.copy)
+        w_turn(2, nc.vector.tensor_copy)
+        nc.vector.quantize_mx(
+            out=w_cod[:, 0:512].bitcast(FP8X4), scales=w_scl[:, 0:512], in_=w_grp[:, 0:1024].bitcast(BF16)
+        )
+        nc.vector.quantize_mx(
+            out=w_cod[:, 512:768].bitcast(FP8X4), scales=w_scl[:, 512:768], in_=w_grp[:, 1024:1536].bitcast(BF16)
+        )
+        bias_product_turn()
+
+        for i in range(1, FINE + 1):
+            load_x(i + NB - 1, False)
+            new_batch(i)
+            for j in range(6):
+                transpose_bank(i, j)
+            if i == 1:
+                bias_product_multiply()
+            mx(i - 1, 0)
+            mx(i - 1, 1)
+            quantise(i, 0, 512)
+            quantise(i, 512, 512)
+            weigh_and_fold(i - 1, 0)
+            quantise(i, 1024, 512)
+            weigh_and_fold(i - 1, 1)
+            if i == 3:
+                finish(0, 2, q1_of[0][:], 8, nc.gpsimd)
+
+        for i in range(FINE + 1, B + 2):
+            if i < B:
+                if i + NB - 1 < B:
+                    load_x(i + NB - 1, False)
+                new_batch(i)
+                for j in range(6):
+                    transpose_bank(i, j)
+            if i >= FINE + 2:
+                mx(i - 2, 0)
+                mx(i - 2, 1)
+                if i <= B:
+                    quantise(i - 1, 0, 1024)
+                    quantise(i - 1, 1024, 512)
+                if i == B + 1:
+                    finish(B - 2, 1, pr_of[B - 2][:], E, nc.gpsimd)
+                weigh_and_fold(i - 2, 0)
+                weigh_and_fold(i - 2, 1)
+                if i == B:
+                    finish_on_gpsimd(i - 4)
+                elif i % 2 == 0:
+                    finish(i - 4, 2, q1_of[(i - 4) // 2][:], 8, nc.gpsimd)
+        finish(B - 1, 1, pr_of[B - 1][:], E, nc.vector)

@@ -171,7 +171,6 @@ def tile_dygcn_pb_t_kernel(tc, x_g, emb, weights_pool, bias_pool, out):
             for c in range(8):
                 nc.tensor.transpose(tpb[:, P * c : P * c + P], g_bf[:, P * c : P * c + P], ident_b[:])
             nc.scalar.copy(out=g_t[:], in_=tpb[:])
-            nc.vector.tensor_copy(out=g_32[:].rearrange("p t e -> p (t e)"), in_=g_bf[:])
 
         def bias_product_multiply():
             for half in range(2):
@@ -231,20 +230,22 @@ def tile_dygcn_pb_t_kernel(tc, x_g, emb, weights_pool, bias_pool, out):
         nc.vector.quantize_mx(
             out=w_cod[:, 512:768].bitcast(FP8X4), scales=w_scl[:, 512:768], in_=w_grp[:, 1024:1536].bitcast(BF16)
         )
-        bias_product_turn()
+        nc.vector.tensor_copy(out=g_32[:].rearrange("p t e -> p (t e)"), in_=g_bf[:])
 
         for i in range(1, FINE + 1):
             load_x(i + NB - 1, False)
             new_batch(i)
-            for j in range(6):
-                transpose_bank(i, j)
-            if i == 1:
+            for h in range(2):
+                for j in range(3 * h, 3 * h + 3):
+                    transpose_bank(i, j)
+                mx(i - 1, h)
+            if i == 2:
+                bias_product_turn()
+            if i == 3:
                 bias_product_multiply()
-            mx(i - 1, 0)
-            mx(i - 1, 1)
             quantise(i, 0, 512)
-            quantise(i, 512, 512)
             weigh_and_fold(i - 1, 0)
+            quantise(i, 512, 512)
             quantise(i, 1024, 512)
             weigh_and_fold(i - 1, 1)
             if i == 3:
@@ -255,17 +256,20 @@ def tile_dygcn_pb_t_kernel(tc, x_g, emb, weights_pool, bias_pool, out):
                 if i + NB - 1 < B:
                     load_x(i + NB - 1, False)
                 new_batch(i)
-                for j in range(6):
-                    transpose_bank(i, j)
+            for h in range(2):
+                if i < B:
+                    for j in range(3 * h, 3 * h + 3):
+                        transpose_bank(i, j)
+                if i >= FINE + 2:
+                    mx(i - 2, h)
             if i >= FINE + 2:
-                mx(i - 2, 0)
-                mx(i - 2, 1)
                 if i <= B:
                     quantise(i - 1, 0, 1024)
-                    quantise(i - 1, 1024, 512)
                 if i == B + 1:
                     finish(B - 2, 1, pr_of[B - 2][:], E, nc.gpsimd)
                 weigh_and_fold(i - 2, 0)
+                if i <= B:
+                    quantise(i - 1, 1024, 512)
                 weigh_and_fold(i - 2, 1)
                 if i == B:
                     finish_on_gpsimd(i - 4)

@@ -20,6 +20,8 @@ NB = 6
 BO = NT * O
 GP_LAST = B - 3
 FINE = 3
+ORD_FIRST = 3
+ORD_0, ORD_N = 2, 3
 
 FLOPS = 2 * B * N * KC * F * E * O + 4 * B * N * E * O
 
@@ -32,6 +34,7 @@ def tile_dygcn_pb_t_kernel(tc, x_g, emb, weights_pool, bias_pool, out):
         gpool = ctx.enter_context(tc.tile_pool(name="gpool", bufs=3))
         cpool = ctx.enter_context(tc.tile_pool(name="cpool", bufs=3))
         ppool = ctx.enter_context(tc.tile_pool(name="ppool", bufs=4))
+        opool = ctx.enter_context(tc.tile_pool(name="opool", bufs=2))
         ps_t = ctx.enter_context(tc.psum_pool(name="ps_t", bufs=6))
         ps_z = ctx.enter_context(tc.psum_pool(name="ps_z", bufs=2))
         ctx.enter_context(tc.manual_schedule())
@@ -50,6 +53,7 @@ def tile_dygcn_pb_t_kernel(tc, x_g, emb, weights_pool, bias_pool, out):
         o_sb = const.tile([P, B * BO], F32, name="o_sb")
 
         xs_of = {}
+        xo_of = {}
         gr_of = {}
         cd_of = {}
         sc_of = {}
@@ -73,12 +77,28 @@ def tile_dygcn_pb_t_kernel(tc, x_g, emb, weights_pool, bias_pool, out):
             cd_of[b] = cpool.tile([P, UNITS * P], U32, name="cd", align_bytes=64)
             sc_of[b] = cpool.tile([P, UNITS * P], U8, name="sc", align_bytes=64)
 
+        def order_words(b):
+            if not ORD_FIRST <= b < B:
+                return
+            xo = opool.tile([P, ORD_N * 512], F32, name="xo")
+            xo_of[b] = xo
+            nc.vector.tensor_copy(
+                out=xo[:].rearrange("p (a u m) -> p a u m", u=2, m=P),
+                in_=xs_of[b][:].bitcast(F32)[:, 512 * ORD_0 : 512 * (ORD_0 + ORD_N)].rearrange(
+                    "p (a m u) -> p a u m", u=2, m=P
+                ),
+            )
+
         def transpose_bank(b, j):
             xw = xs_of[b][:].bitcast(F32)
             tp = ps_t.tile([P, 512], F32, name="tp", tag="tp")
             for s in range(4):
                 c0 = 256 * (2 * j + s // 2)
-                nc.tensor.transpose(tp[:, P * s : P * s + P], xw[:, c0 + s % 2 : c0 + 256 : 2], ident_f[:])
+                words = xw[:, c0 + s % 2 : c0 + 256 : 2]
+                if b in xo_of and ORD_0 <= j < ORD_0 + ORD_N:
+                    c0 = 512 * (j - ORD_0) + P * s
+                    words = xo_of[b][:, c0 : c0 + P]
+                nc.tensor.transpose(tp[:, P * s : P * s + P], words, ident_f[:])
             nc.scalar.copy(
                 out=gr_of[b][:, 512 * j : 512 * j + 512].rearrange("p (a n u) -> p a n u", a=2, u=2),
                 in_=tp[:].rearrange("p (a u n) -> p a n u", a=2, u=2),
@@ -246,6 +266,7 @@ def tile_dygcn_pb_t_kernel(tc, x_g, emb, weights_pool, bias_pool, out):
             quantise(i, 0, 512)
             weigh_and_fold(i - 1, 0)
             quantise(i, 512, 512)
+            order_words(i + 1)
             quantise(i, 1024, 512)
             weigh_and_fold(i - 1, 1)
             if i == 3:
@@ -262,12 +283,15 @@ def tile_dygcn_pb_t_kernel(tc, x_g, emb, weights_pool, bias_pool, out):
                         transpose_bank(i, j)
                 if i >= FINE + 2:
                     mx(i - 2, h)
+            if i == FINE + 1:
+                order_words(i + 1)
             if i >= FINE + 2:
                 if i <= B:
                     quantise(i - 1, 0, 1024)
                 if i == B + 1:
                     finish(B - 2, 1, pr_of[B - 2][:], E, nc.gpsimd)
                 weigh_and_fold(i - 2, 0)
+                order_words(i + 1)
                 if i <= B:
                     quantise(i - 1, 1024, 512)
                 weigh_and_fold(i - 2, 1)

@@ -21,7 +21,7 @@ BO = NT * O
 GP_LAST = B - 3
 FINE = 3
 ORD_FIRST = 3
-ORD_0, ORD_N = 2, 3
+ORD_0, ORD_N = 2, 2
 
 FLOPS = 2 * B * N * KC * F * E * O + 4 * B * N * E * O
 
@@ -82,7 +82,7 @@ def tile_dygcn_pb_t_kernel(tc, x_g, emb, weights_pool, bias_pool, out):
                 return
             xo = opool.tile([P, ORD_N * 512], F32, name="xo")
             xo_of[b] = xo
-            nc.vector.tensor_copy(
+            nc.scalar.copy(
                 out=xo[:].rearrange("p (a u m) -> p a u m", u=2, m=P),
                 in_=xs_of[b][:].bitcast(F32)[:, 512 * ORD_0 : 512 * (ORD_0 + ORD_N)].rearrange(
                     "p (a m u) -> p a u m", u=2, m=P
@@ -258,6 +258,8 @@ def tile_dygcn_pb_t_kernel(tc, x_g, emb, weights_pool, bias_pool, out):
             for h in range(2):
                 for j in range(3 * h, 3 * h + 3):
                     transpose_bank(i, j)
+                if h == 0:
+                    order_words(i + 1)
                 mx(i - 1, h)
             if i == 2:
                 bias_product_turn()
@@ -266,7 +268,6 @@ def tile_dygcn_pb_t_kernel(tc, x_g, emb, weights_pool, bias_pool, out):
             quantise(i, 0, 512)
             weigh_and_fold(i - 1, 0)
             quantise(i, 512, 512)
-            order_words(i + 1)
             quantise(i, 1024, 512)
             weigh_and_fold(i - 1, 1)
             if i == 3:
@@ -281,17 +282,16 @@ def tile_dygcn_pb_t_kernel(tc, x_g, emb, weights_pool, bias_pool, out):
                 if i < B:
                     for j in range(3 * h, 3 * h + 3):
                         transpose_bank(i, j)
+                if h == 0:
+                    order_words(i + 1)
                 if i >= FINE + 2:
                     mx(i - 2, h)
-            if i == FINE + 1:
-                order_words(i + 1)
             if i >= FINE + 2:
                 if i <= B:
                     quantise(i - 1, 0, 1024)
                 if i == B + 1:
                     finish(B - 2, 1, pr_of[B - 2][:], E, nc.gpsimd)
                 weigh_and_fold(i - 2, 0)
-                order_words(i + 1)
                 if i <= B:
                     quantise(i - 1, 1024, 512)
                 weigh_and_fold(i - 2, 1)

@@ -18,7 +18,6 @@ NT = N // P
 UNITS = KC * NT
 NB = 6
 BO = NT * O
-GP_LAST = B - 3
 FINE = 3
 ORD_FIRST = 3
 ORD_0, ORD_N = 2, 2
@@ -59,7 +58,7 @@ def tile_dygcn_pb_t_kernel(tc, x_g, emb, weights_pool, bias_pool, out):
         sc_of = {}
         zp_of = {}
         pr_of = {}
-        q1_of = {}
+        rs_of = {}
 
         def load_x(b, split):
             xs = xpool.tile([P, KC * NT * F], BF16, name="xs")
@@ -140,50 +139,25 @@ def tile_dygcn_pb_t_kernel(tc, x_g, emb, weights_pool, bias_pool, out):
                 op=MULT,
             )
 
-        def fold_16_to_8(b, h):
-            if h == 0 and b % 2 == 0:
-                q1_of[b // 2] = ppool.tile([P, 2 * BO * 8], F32, name="q1")
-            pv = pr_of[b][:, 512 * h : 512 * h + 512].rearrange("p (c e) -> p c e", e=E)
-            c0 = 512 * (b % 2) + 256 * h
-            nc.gpsimd.tensor_tensor(
-                out=q1_of[b // 2][:, c0 : c0 + 256].rearrange("p (c e) -> p c e", e=8),
-                in0=pv[:, :, 0:8],
-                in1=pv[:, :, 8:16],
-                op=ADD,
-            )
-
-        def finish(b0, nb, terms, width, adder):
-            rs = ppool.tile([P, 2 * BO], F32, name="rs")
+        def finish(b, adder):
+            if b % 2 == 0:
+                rs_of[b // 2] = ppool.tile([P, 2 * BO], F32, name="rs")
+            rs = rs_of[b // 2][:, BO * (b % 2) : BO * (b % 2) + BO]
             nc.vector.tensor_reduce(
-                out=rs[:, 0 : nb * BO], in_=terms.rearrange("p (c e) -> p c e", e=width), axis=AX, op=ADD
+                out=rs, in_=pr_of[b][:].rearrange("p (c e) -> p c e", e=E), axis=AX, op=ADD
             )
-            cols = slice(BO * b0, BO * (b0 + nb))
-            adder.tensor_tensor(out=o_sb[:, cols], in0=rs[:, 0 : nb * BO], in1=gb[:, cols], op=ADD)
+            cols = slice(BO * b, BO * (b + 1))
+            adder.tensor_tensor(out=o_sb[:, cols], in0=rs, in1=gb[:, cols], op=ADD)
+            if b >= B - 2:
+                first, count = b, 1
+            elif b % 2 == 1:
+                first, count = b - 1, 2
+            else:
+                return
+            cols = slice(BO * first, BO * (first + count))
             nc.sync.dma_start(
-                out=out[b0 : b0 + nb].rearrange("b (p t) o -> p b (t o)", t=NT),
-                in_=o_sb[:, cols].rearrange("p (b c) -> p b c", b=nb),
-            )
-
-        def finish_on_gpsimd(b0):
-            terms = q1_of[b0 // 2][:]
-            width = 8
-            while width > 1:
-                half = width // 2
-                tv = terms.rearrange("p (c e) -> p c e", e=width)
-                nxt = ppool.tile([P, 2 * BO * half], F32, name="fold%d" % half)
-                nc.gpsimd.tensor_tensor(
-                    out=nxt[:].rearrange("p (c e) -> p c e", e=half),
-                    in0=tv[:, :, 0:half],
-                    in1=tv[:, :, half:width],
-                    op=ADD,
-                )
-                terms = nxt[:]
-                width = half
-            cols = slice(BO * b0, BO * (b0 + 2))
-            nc.gpsimd.tensor_tensor(out=o_sb[:, cols], in0=terms, in1=gb[:, cols], op=ADD)
-            nc.sync.dma_start(
-                out=out[b0 : b0 + 2].rearrange("b (p t) o -> p b (t o)", t=NT),
-                in_=o_sb[:, cols].rearrange("p (b c) -> p b c", b=2),
+                out=out[first : first + count].rearrange("b (p t) o -> p b (t o)", t=NT),
+                in_=o_sb[:, cols].rearrange("p (b c) -> p b c", b=count),
             )
 
         def bias_product_turn():
@@ -205,11 +179,6 @@ def tile_dygcn_pb_t_kernel(tc, x_g, emb, weights_pool, bias_pool, out):
                         stop=True,
                     )
                 nc.scalar.copy(out=gb[:, 512 * half : 512 * half + 512], in_=gp[:])
-
-        def weigh_and_fold(b, h):
-            weigh(b, h)
-            if b <= GP_LAST:
-                fold_16_to_8(b, h)
 
         make_identity(nc, ident_f[:])
         make_identity(nc, ident_b[:])
@@ -266,12 +235,13 @@ def tile_dygcn_pb_t_kernel(tc, x_g, emb, weights_pool, bias_pool, out):
             if i == 3:
                 bias_product_multiply()
             quantise(i, 0, 512)
-            weigh_and_fold(i - 1, 0)
+            weigh(i - 1, 0)
             quantise(i, 512, 512)
             quantise(i, 1024, 512)
-            weigh_and_fold(i - 1, 1)
+            weigh(i - 1, 1)
             if i == 3:
-                finish(0, 2, q1_of[0][:], 8, nc.gpsimd)
+                finish(0, nc.gpsimd)
+                finish(1, nc.gpsimd)
 
         for i in range(FINE + 1, B + 2):
             if i < B:
@@ -289,14 +259,9 @@ def tile_dygcn_pb_t_kernel(tc, x_g, emb, weights_pool, bias_pool, out):
             if i >= FINE + 2:
                 if i <= B:
                     quantise(i - 1, 0, 1024)
-                if i == B + 1:
-                    finish(B - 2, 1, pr_of[B - 2][:], E, nc.gpsimd)
-                weigh_and_fold(i - 2, 0)
+                finish(i - 3, nc.gpsimd)
+                weigh(i - 2, 0)
                 if i <= B:
                     quantise(i - 1, 1024, 512)
-                weigh_and_fold(i - 2, 1)
-                if i == B:
-                    finish_on_gpsimd(i - 4)
-                elif i % 2 == 0:
-                    finish(i - 4, 2, q1_of[(i - 4) // 2][:], 8, nc.gpsimd)
-        finish(B - 1, 1, pr_of[B - 1][:], E, nc.vector)
+                weigh(i - 2, 1)
+        finish(B - 1, nc.vector)

@@ -18,9 +18,9 @@ NT = N // P
 UNITS = KC * NT
 NB = 6
 BO = NT * O
-FINE = 3
-ORD_FIRST = 3
-ORD_0, ORD_N = 2, 2
+SPLIT = 3
+EMB_FIRST = 4
+ORD_FIRST = 5
 
 FLOPS = 2 * B * N * KC * F * E * O + 4 * B * N * E * O
 
@@ -33,6 +33,7 @@ def tile_dygcn_pb_t_kernel(tc, x_g, emb, weights_pool, bias_pool, out):
         gpool = ctx.enter_context(tc.tile_pool(name="gpool", bufs=3))
         cpool = ctx.enter_context(tc.tile_pool(name="cpool", bufs=3))
         ppool = ctx.enter_context(tc.tile_pool(name="ppool", bufs=4))
+        qpool = ctx.enter_context(tc.tile_pool(name="qpool", bufs=7))
         opool = ctx.enter_context(tc.tile_pool(name="opool", bufs=2))
         ps_t = ctx.enter_context(tc.psum_pool(name="ps_t", bufs=6))
         ps_z = ctx.enter_context(tc.psum_pool(name="ps_z", bufs=2))
@@ -58,6 +59,7 @@ def tile_dygcn_pb_t_kernel(tc, x_g, emb, weights_pool, bias_pool, out):
         sc_of = {}
         zp_of = {}
         pr_of = {}
+        q1_of = {}
         rs_of = {}
 
         def load_x(b, split):
@@ -71,22 +73,37 @@ def tile_dygcn_pb_t_kernel(tc, x_g, emb, weights_pool, bias_pool, out):
             else:
                 nc.sync.dma_start(out=dst, in_=src)
 
+        def load_emb(b0, b1):
+            nc.sync.dma_start(
+                out=g_bf[:].rearrange("p (b c) -> p b c", b=B)[:, b0:b1],
+                in_=emb.rearrange("b (p t) e -> p b (t e)", t=NT)[:, b0:b1],
+            )
+
+        def emb_to_float32(b0, b1):
+            nc.vector.tensor_copy(
+                out=g_32[:, NT * b0 : NT * b1, :].rearrange("p t e -> p (t e)"),
+                in_=g_bf[:, NT * E * b0 : NT * E * b1],
+            )
+
         def new_batch(b):
             gr_of[b] = gpool.tile([P, UNITS * 256], F32, name="gr", align_bytes=64)
             cd_of[b] = cpool.tile([P, UNITS * P], U32, name="cd", align_bytes=64)
             sc_of[b] = cpool.tile([P, UNITS * P], U8, name="sc", align_bytes=64)
 
-        def order_words(b):
+        def order_words(b, j, banks, copy):
             if not ORD_FIRST <= b < B:
                 return
-            xo = opool.tile([P, ORD_N * 512], F32, name="xo")
-            xo_of[b] = xo
-            nc.scalar.copy(
+            xo = opool.tile([P, banks * 512], F32, name="xo%d" % j)
+            for d in range(banks):
+                xo_of[(b, j + d)] = xo[:, 512 * d : 512 * d + 512]
+            copy(
                 out=xo[:].rearrange("p (a u m) -> p a u m", u=2, m=P),
-                in_=xs_of[b][:].bitcast(F32)[:, 512 * ORD_0 : 512 * (ORD_0 + ORD_N)].rearrange(
-                    "p (a m u) -> p a u m", u=2, m=P
-                ),
+                in_=xs_of[b][:].bitcast(F32)[:, 512 * j : 512 * (j + banks)].rearrange("p (a m u) -> p a u m", u=2, m=P),
             )
+
+        def order_on_vector(b):
+            order_words(b, 1, 2, nc.vector.tensor_copy)
+            order_words(b, 4, 1, nc.vector.tensor_copy)
 
         def transpose_bank(b, j):
             xw = xs_of[b][:].bitcast(F32)
@@ -94,9 +111,8 @@ def tile_dygcn_pb_t_kernel(tc, x_g, emb, weights_pool, bias_pool, out):
             for s in range(4):
                 c0 = 256 * (2 * j + s // 2)
                 words = xw[:, c0 + s % 2 : c0 + 256 : 2]
-                if b in xo_of and ORD_0 <= j < ORD_0 + ORD_N:
-                    c0 = 512 * (j - ORD_0) + P * s
-                    words = xo_of[b][:, c0 : c0 + P]
+                if (b, j) in xo_of:
+                    words = xo_of[(b, j)][:, P * s : P * s + P]
                 nc.tensor.transpose(tp[:, P * s : P * s + P], words, ident_f[:])
             nc.scalar.copy(
                 out=gr_of[b][:, 512 * j : 512 * j + 512].rearrange("p (a n u) -> p a n u", a=2, u=2),
@@ -113,7 +129,10 @@ def tile_dygcn_pb_t_kernel(tc, x_g, emb, weights_pool, bias_pool, out):
         def mx(b, h):
             cd = cd_of[b]
             sc = sc_of[b]
-            zp = ps_z.tile([P, 512], F32, name="zp", tag="zp")
+            if b < B - 2:
+                zp = ps_z.tile([P, 512], F32, name="zp", tag="zp")
+            else:
+                zp = ps_t.tile([P, 512], F32, name="zp", tag="tp")
             zp_of[(b, h)] = zp
             for a in range(2):
                 for k in range(KC):
@@ -139,26 +158,55 @@ def tile_dygcn_pb_t_kernel(tc, x_g, emb, weights_pool, bias_pool, out):
                 op=MULT,
             )
 
-        def finish(b, adder):
-            if b % 2 == 0:
-                rs_of[b // 2] = ppool.tile([P, 2 * BO], F32, name="rs")
-            rs = rs_of[b // 2][:, BO * (b % 2) : BO * (b % 2) + BO]
-            nc.vector.tensor_reduce(
-                out=rs, in_=pr_of[b][:].rearrange("p (c e) -> p c e", e=E), axis=AX, op=ADD
+        def fold_16_to_8(b, h):
+            if h == 0:
+                q1_of[b] = qpool.tile([P, BO * 8], F32, name="q1")
+            pv = pr_of[b][:, 512 * h : 512 * h + 512].rearrange("p (c e) -> p c e", e=E)
+            nc.gpsimd.tensor_tensor(
+                out=q1_of[b][:, 256 * h : 256 * h + 256].rearrange("p (c e) -> p c e", e=8),
+                in0=pv[:, :, 0:8],
+                in1=pv[:, :, 8:16],
+                op=ADD,
             )
+
+        def weigh_and_fold(b, h):
+            weigh(b, h)
+            if b < B - 1:
+                fold_16_to_8(b, h)
+
+        def add_bias(b, sums, adder):
             cols = slice(BO * b, BO * (b + 1))
-            adder.tensor_tensor(out=o_sb[:, cols], in0=rs, in1=gb[:, cols], op=ADD)
-            if b >= B - 2:
-                first, count = b, 1
-            elif b % 2 == 1:
-                first, count = b - 1, 2
-            else:
-                return
-            cols = slice(BO * first, BO * (first + count))
-            nc.sync.dma_start(
-                out=out[first : first + count].rearrange("b (p t) o -> p b (t o)", t=NT),
+            adder.tensor_tensor(out=o_sb[:, cols], in0=sums, in1=gb[:, cols], op=ADD)
+
+        def store(b0, count, queue):
+            cols = slice(BO * b0, BO * (b0 + count))
+            queue.dma_start(
+                out=out[b0 : b0 + count].rearrange("b (p t) o -> p b (t o)", t=NT),
                 in_=o_sb[:, cols].rearrange("p (b c) -> p b c", b=count),
             )
+
+        def finish(b, adder):
+            terms, width = (q1_of[b], 8) if b in q1_of else (pr_of[b], E)
+            rs = ppool.tile([P, BO], F32, name="rs")
+            nc.vector.tensor_reduce(
+                out=rs[:], in_=terms[:].rearrange("p (c e) -> p c e", e=width), axis=AX, op=ADD
+            )
+            add_bias(b, rs[:], adder)
+
+        def finish_on_gpsimd(b):
+            terms, width = q1_of[b][:], 8
+            while width > 1:
+                half = width // 2
+                tv = terms.rearrange("p (c e) -> p c e", e=width)
+                nxt = ppool.tile([P, BO * half], F32, name="fold%d" % half)
+                nc.gpsimd.tensor_tensor(
+                    out=nxt[:].rearrange("p (c e) -> p c e", e=half),
+                    in0=tv[:, :, 0:half],
+                    in1=tv[:, :, half:width],
+                    op=ADD,
+                )
+                terms, width = nxt[:], half
+            add_bias(b, terms, nc.gpsimd)
 
         def bias_product_turn():
             tpb = ps_t.tile([P, 1024], BF16, name="tpb", tag="tp")
@@ -192,12 +240,11 @@ def tile_dygcn_pb_t_kernel(tc, x_g, emb, weights_pool, bias_pool, out):
                 out=w_raw[:].rearrange("p (k e c) -> p k e c", k=KC, e=E)[:, k],
                 in_=weights_pool.rearrange("e k (p t) o -> p k e (t o)", t=4)[:, k],
             )
-        nc.sync.dma_start(
-            out=g_bf[:].rearrange("p (b c) -> p b c", b=B),
-            in_=emb.rearrange("b (p t) e -> p b (t e)", t=NT),
-        )
         for b in range(1, NB):
-            load_x(b, b <= FINE)
+            load_x(b, b <= SPLIT)
+            if b == 1:
+                load_emb(0, EMB_FIRST)
+        load_emb(EMB_FIRST, B)
 
         def w_turn(k, copy):
             copy(
@@ -205,63 +252,65 @@ def tile_dygcn_pb_t_kernel(tc, x_g, emb, weights_pool, bias_pool, out):
                 in_=w_raw[:, 1024 * k : 1024 * k + 1024].rearrange("p (e t o) -> p o e t", e=E, t=4),
             )
 
-        new_batch(0)
-        for k in range(KC):
-            transpose_bank(0, 2 * k)
-            transpose_bank(0, 2 * k + 1)
-            quantise(0, 512 * k, 512)
-        w_turn(0, nc.vector.tensor_copy)
-        w_turn(1, nc.scalar.copy)
-        w_turn(2, nc.vector.tensor_copy)
-        nc.vector.quantize_mx(
-            out=w_cod[:, 0:512].bitcast(FP8X4), scales=w_scl[:, 0:512], in_=w_grp[:, 0:1024].bitcast(BF16)
-        )
-        nc.vector.quantize_mx(
-            out=w_cod[:, 512:768].bitcast(FP8X4), scales=w_scl[:, 512:768], in_=w_grp[:, 1024:1536].bitcast(BF16)
-        )
-        nc.vector.tensor_copy(out=g_32[:].rearrange("p t e -> p (t e)"), in_=g_bf[:])
-
-        for i in range(1, FINE + 1):
-            load_x(i + NB - 1, False)
-            new_batch(i)
-            for h in range(2):
-                for j in range(3 * h, 3 * h + 3):
-                    transpose_bank(i, j)
-                if h == 0:
-                    order_words(i + 1)
-                mx(i - 1, h)
-            if i == 2:
-                bias_product_turn()
-            if i == 3:
-                bias_product_multiply()
-            quantise(i, 0, 512)
-            weigh(i - 1, 0)
-            quantise(i, 512, 512)
-            quantise(i, 1024, 512)
-            weigh(i - 1, 1)
-            if i == 3:
-                finish(0, nc.gpsimd)
-                finish(1, nc.gpsimd)
-
-        for i in range(FINE + 1, B + 2):
+        for i in range(B + 3):
             if i < B:
-                if i + NB - 1 < B:
+                if i > 0 and i + NB - 1 < B:
                     load_x(i + NB - 1, False)
                 new_batch(i)
+            if i == 6:
+                bias_product_turn()
+            if i == 7:
+                bias_product_multiply()
             for h in range(2):
                 if i < B:
                     for j in range(3 * h, 3 * h + 3):
                         transpose_bank(i, j)
-                if h == 0:
-                    order_words(i + 1)
-                if i >= FINE + 2:
+                        if j == 2:
+                            order_words(i + 1, 5, 1, nc.scalar.copy)
+                if 2 <= i < B + 2:
                     mx(i - 2, h)
-            if i >= FINE + 2:
-                if i <= B:
-                    quantise(i - 1, 0, 1024)
-                finish(i - 3, nc.gpsimd)
-                weigh(i - 2, 0)
-                if i <= B:
-                    quantise(i - 1, 1024, 512)
-                weigh(i - 2, 1)
+            if i == 0:
+                quantise(0, 0, 512)
+                quantise(0, 512, 512)
+                quantise(0, 1024, 512)
+                w_turn(0, nc.vector.tensor_copy)
+                w_turn(1, nc.scalar.copy)
+                w_turn(2, nc.vector.tensor_copy)
+                for c0, c1 in ((0, 512), (512, 768)):
+                    nc.vector.quantize_mx(
+                        out=w_cod[:, c0:c1].bitcast(FP8X4),
+                        scales=w_scl[:, c0:c1],
+                        in_=w_grp[:, 2 * c0 : 2 * c1].bitcast(BF16),
+                    )
+            if i == 2:
+                emb_to_float32(0, EMB_FIRST)
+            if i >= 3:
+                weigh_and_fold(i - 3, 0)
+                if i == B:
+                    finish(B - 4, nc.gpsimd)
+                    quantise(B - 1, 0, 1024)
+                    quantise(B - 1, 1024, 512)
+                weigh_and_fold(i - 3, 1)
+            if i == 6:
+                emb_to_float32(EMB_FIRST, B)
+            if 7 <= i < 10:
+                done = (2 * i - 14, 2 * i - 13)
+            elif 10 <= i < B or i == B + 1:
+                done = (i - 4,)
+            else:
+                done = ()
+            for b in done:
+                finish(b, nc.gpsimd)
+                if b % 2 == 1:
+                    store(b - 1, 2, nc.sync)
+            if 5 <= i < B:
+                order_on_vector(i + 1)
+            if 2 <= i < B:
+                quantise(i - 1, 0, 1024)
+                quantise(i - 1, 1024, 512)
+            if i < 5:
+                order_on_vector(i + 1)
+        finish_on_gpsimd(B - 2)
+        store(B - 2, 1, nc.sync)
         finish(B - 1, nc.vector)
+        store(B - 1, 1, nc.scalar)

@@ -20,7 +20,8 @@ NB = 6
 BO = NT * O
 SPLIT = 3
 EMB_FIRST = 4
-ORD_FIRST = 5
+ORD_FIRST = 6
+ORD_UNITS = (2, 2, 1)
 
 FLOPS = 2 * B * N * KC * F * E * O + 4 * B * N * E * O
 
@@ -90,29 +91,27 @@ def tile_dygcn_pb_t_kernel(tc, x_g, emb, weights_pool, bias_pool, out):
             cd_of[b] = cpool.tile([P, UNITS * P], U32, name="cd", align_bytes=64)
             sc_of[b] = cpool.tile([P, UNITS * P], U8, name="sc", align_bytes=64)
 
-        def order_words(b, j, banks, copy):
+        def order_words(b, u0, units):
             if not ORD_FIRST <= b < B:
                 return
-            xo = opool.tile([P, banks * 512], F32, name="xo%d" % j)
-            for d in range(banks):
-                xo_of[(b, j + d)] = xo[:, 512 * d : 512 * d + 512]
-            copy(
+            xo = opool.tile([P, units * 256], F32, name="xo%d" % u0)
+            for d in range(units):
+                xo_of[(b, u0 + d)] = xo[:, 256 * d : 256 * d + 256]
+            nc.scalar.copy(
                 out=xo[:].rearrange("p (a u m) -> p a u m", u=2, m=P),
-                in_=xs_of[b][:].bitcast(F32)[:, 512 * j : 512 * (j + banks)].rearrange("p (a m u) -> p a u m", u=2, m=P),
+                in_=xs_of[b][:]
+                .bitcast(F32)[:, 256 * u0 : 256 * (u0 + units)]
+                .rearrange("p (a m u) -> p a u m", u=2, m=P),
             )
-
-        def order_on_vector(b):
-            order_words(b, 1, 2, nc.vector.tensor_copy)
-            order_words(b, 4, 1, nc.vector.tensor_copy)
 
         def transpose_bank(b, j):
             xw = xs_of[b][:].bitcast(F32)
             tp = ps_t.tile([P, 512], F32, name="tp", tag="tp")
             for s in range(4):
-                c0 = 256 * (2 * j + s // 2)
-                words = xw[:, c0 + s % 2 : c0 + 256 : 2]
-                if (b, j) in xo_of:
-                    words = xo_of[(b, j)][:, P * s : P * s + P]
+                unit, half = 2 * j + s // 2, s % 2
+                words = xw[:, 256 * unit + half : 256 * unit + 256 : 2]
+                if (b, unit) in xo_of:
+                    words = xo_of[(b, unit)][:, P * half : P * half + P]
                 nc.tensor.transpose(tp[:, P * s : P * s + P], words, ident_f[:])
             nc.scalar.copy(
                 out=gr_of[b][:, 512 * j : 512 * j + 512].rearrange("p (a n u) -> p a n u", a=2, u=2),
@@ -126,26 +125,28 @@ def tile_dygcn_pb_t_kernel(tc, x_g, emb, weights_pool, bias_pool, out):
                 in_=gr_of[b][:, 2 * c0 : 2 * (c0 + cw)].bitcast(BF16),
             )
 
-        def mx(b, h):
+        def mx_third(b, third):
             cd = cd_of[b]
             sc = sc_of[b]
-            if b < B - 2:
-                zp = ps_z.tile([P, 512], F32, name="zp", tag="zp")
-            else:
-                zp = ps_t.tile([P, 512], F32, name="zp", tag="tp")
-            zp_of[(b, h)] = zp
-            for a in range(2):
-                for k in range(KC):
-                    c0 = P * (NT * k + 2 * h + a)
-                    nc.tensor.matmul_mx(
-                        out=zp[:, 256 * a : 256 * a + 256],
-                        lhsT=cd[:, c0 : c0 + P].bitcast(FP8X4),
-                        lhsT_scale=sc[:, c0 : c0 + P],
-                        rhs=w_cod[:, 256 * k : 256 * k + 256].bitcast(FP8X4),
-                        rhs_scale=w_scl[:, 256 * k : 256 * k + 256],
-                        start=(k == 0),
-                        stop=(k == KC - 1),
-                    )
+            for n in range(4 * third, 4 * third + 4):
+                t, k = n // KC, n % KC
+                h, a = t // 2, t % 2
+                if a == 0 and k == 0:
+                    if b < B - 2:
+                        zp = ps_z.tile([P, 512], F32, name="zp", tag="zp")
+                    else:
+                        zp = ps_t.tile([P, 512], F32, name="zp", tag="tp")
+                    zp_of[(b, h)] = zp
+                c0 = P * (NT * k + t)
+                nc.tensor.matmul_mx(
+                    out=zp_of[(b, h)][:, 256 * a : 256 * a + 256],
+                    lhsT=cd[:, c0 : c0 + P].bitcast(FP8X4),
+                    lhsT_scale=sc[:, c0 : c0 + P],
+                    rhs=w_cod[:, 256 * k : 256 * k + 256].bitcast(FP8X4),
+                    rhs_scale=w_scl[:, 256 * k : 256 * k + 256],
+                    start=(k == 0),
+                    stop=(k == KC - 1),
+                )
 
         def weigh(b, h):
             if h == 0:
@@ -171,29 +172,30 @@ def tile_dygcn_pb_t_kernel(tc, x_g, emb, weights_pool, bias_pool, out):
 
         def weigh_and_fold(b, h):
             weigh(b, h)
-            if b < B - 1:
+            if B - 3 <= b < B - 1:
                 fold_16_to_8(b, h)
 
-        def add_bias(b, sums, adder):
-            cols = slice(BO * b, BO * (b + 1))
-            adder.tensor_tensor(out=o_sb[:, cols], in0=sums, in1=gb[:, cols], op=ADD)
+        def reduce(b):
+            terms, width = (q1_of[b], 8) if b in q1_of else (pr_of[b], E)
+            if b // 2 not in rs_of:
+                rs_of[b // 2] = ppool.tile([P, 2 * BO], F32, name="rs")
+            c0 = BO * (b % 2)
+            nc.vector.tensor_reduce(
+                out=rs_of[b // 2][:, c0 : c0 + BO],
+                in_=terms[:].rearrange("p (c e) -> p c e", e=width),
+                axis=AX,
+                op=ADD,
+            )
 
-        def store(b0, count, queue):
+        def finish(b0, count, sums, adder, queue):
             cols = slice(BO * b0, BO * (b0 + count))
+            adder.tensor_tensor(out=o_sb[:, cols], in0=sums, in1=gb[:, cols], op=ADD)
             queue.dma_start(
                 out=out[b0 : b0 + count].rearrange("b (p t) o -> p b (t o)", t=NT),
                 in_=o_sb[:, cols].rearrange("p (b c) -> p b c", b=count),
             )
 
-        def finish(b, adder):
-            terms, width = (q1_of[b], 8) if b in q1_of else (pr_of[b], E)
-            rs = ppool.tile([P, BO], F32, name="rs")
-            nc.vector.tensor_reduce(
-                out=rs[:], in_=terms[:].rearrange("p (c e) -> p c e", e=width), axis=AX, op=ADD
-            )
-            add_bias(b, rs[:], adder)
-
-        def finish_on_gpsimd(b):
+        def sum_on_gpsimd(b):
             terms, width = q1_of[b][:], 8
             while width > 1:
                 half = width // 2
@@ -206,7 +208,7 @@ def tile_dygcn_pb_t_kernel(tc, x_g, emb, weights_pool, bias_pool, out):
                     op=ADD,
                 )
                 terms, width = nxt[:], half
-            add_bias(b, terms, nc.gpsimd)
+            return terms
 
         def bias_product_turn():
             tpb = ps_t.tile([P, 1024], BF16, name="tpb", tag="tp")
@@ -261,14 +263,13 @@ def tile_dygcn_pb_t_kernel(tc, x_g, emb, weights_pool, bias_pool, out):
                 bias_product_turn()
             if i == 7:
                 bias_product_multiply()
-            for h in range(2):
+            for third in range(3):
                 if i < B:
-                    for j in range(3 * h, 3 * h + 3):
-                        transpose_bank(i, j)
-                        if j == 2:
-                            order_words(i + 1, 5, 1, nc.scalar.copy)
+                    transpose_bank(i, 2 * third)
+                    transpose_bank(i, 2 * third + 1)
+                    order_words(i + 1, 4 * third + 2, ORD_UNITS[third])
                 if 2 <= i < B + 2:
-                    mx(i - 2, h)
+                    mx_third(i - 2, third)
             if i == 0:
                 quantise(0, 0, 512)
                 quantise(0, 512, 512)
@@ -287,30 +288,22 @@ def tile_dygcn_pb_t_kernel(tc, x_g, emb, weights_pool, bias_pool, out):
             if i >= 3:
                 weigh_and_fold(i - 3, 0)
                 if i == B:
-                    finish(B - 4, nc.gpsimd)
+                    reduce(B - 4)
                     quantise(B - 1, 0, 1024)
                     quantise(B - 1, 1024, 512)
                 weigh_and_fold(i - 3, 1)
             if i == 6:
                 emb_to_float32(EMB_FIRST, B)
-            if 7 <= i < 10:
-                done = (2 * i - 14, 2 * i - 13)
-            elif 10 <= i < B or i == B + 1:
-                done = (i - 4,)
-            else:
-                done = ()
-            for b in done:
-                finish(b, nc.gpsimd)
-                if b % 2 == 1:
-                    store(b - 1, 2, nc.sync)
-            if 5 <= i < B:
-                order_on_vector(i + 1)
+            if 4 <= i < B or i == B + 1:
+                b = i - 4
+                reduce(b)
+                if b >= 3 and b % 2 == 1:
+                    finish(b - 1, 2, rs_of[b // 2][:], nc.gpsimd, nc.sync)
+                if b == 3:
+                    finish(0, 2, rs_of[0][:], nc.gpsimd, nc.sync)
             if 2 <= i < B:
                 quantise(i - 1, 0, 1024)
                 quantise(i - 1, 1024, 512)
-            if i < 5:
-                order_on_vector(i + 1)
-        finish_on_gpsimd(B - 2)
-        store(B - 2, 1, nc.sync)
-        finish(B - 1, nc.vector)
-        store(B - 1, 1, nc.scalar)
+        finish(B - 2, 1, sum_on_gpsimd(B - 2), nc.gpsimd, nc.sync)
+        reduce(B - 1)
+        finish(B - 1, 1, rs_of[B // 2 - 1][:, BO:], nc.vector, nc.scalar)

@@ -20,8 +20,7 @@ NB = 6
 BO = NT * O
 SPLIT = 3
 EMB_FIRST = 4
-ORD_FIRST = 6
-ORD_UNITS = (2, 2, 1)
+ORD_FIRST = 4
 
 FLOPS = 2 * B * N * KC * F * E * O + 4 * B * N * E * O
 
@@ -91,17 +90,18 @@ def tile_dygcn_pb_t_kernel(tc, x_g, emb, weights_pool, bias_pool, out):
             cd_of[b] = cpool.tile([P, UNITS * P], U32, name="cd", align_bytes=64)
             sc_of[b] = cpool.tile([P, UNITS * P], U8, name="sc", align_bytes=64)
 
-        def order_words(b, u0, units):
+        def order_words(b, u0, units, step, copy):
             if not ORD_FIRST <= b < B:
                 return
-            xo = opool.tile([P, units * 256], F32, name="xo%d" % u0)
+            xo = opool.tile([P, units, 256], F32, name="xo%d" % u0)
             for d in range(units):
-                xo_of[(b, u0 + d)] = xo[:, 256 * d : 256 * d + 256]
-            nc.scalar.copy(
-                out=xo[:].rearrange("p (a u m) -> p a u m", u=2, m=P),
+                xo_of[(b, u0 + step * d)] = xo[:, d, :]
+            copy(
+                out=xo[:].rearrange("p a (u m) -> p a u m", u=2),
                 in_=xs_of[b][:]
-                .bitcast(F32)[:, 256 * u0 : 256 * (u0 + units)]
-                .rearrange("p (a m u) -> p a u m", u=2, m=P),
+                .bitcast(F32)
+                .rearrange("p (c w) -> p c w", w=256)[:, u0 : u0 + step * (units - 1) + 1 : step]
+                .rearrange("p a (m u) -> p a u m", u=2),
             )
 
         def transpose_bank(b, j):
@@ -125,28 +125,24 @@ def tile_dygcn_pb_t_kernel(tc, x_g, emb, weights_pool, bias_pool, out):
                 in_=gr_of[b][:, 2 * c0 : 2 * (c0 + cw)].bitcast(BF16),
             )
 
-        def mx_third(b, third):
-            cd = cd_of[b]
-            sc = sc_of[b]
-            for n in range(4 * third, 4 * third + 4):
-                t, k = n // KC, n % KC
-                h, a = t // 2, t % 2
-                if a == 0 and k == 0:
-                    if b < B - 2:
-                        zp = ps_z.tile([P, 512], F32, name="zp", tag="zp")
-                    else:
-                        zp = ps_t.tile([P, 512], F32, name="zp", tag="tp")
-                    zp_of[(b, h)] = zp
-                c0 = P * (NT * k + t)
-                nc.tensor.matmul_mx(
-                    out=zp_of[(b, h)][:, 256 * a : 256 * a + 256],
-                    lhsT=cd[:, c0 : c0 + P].bitcast(FP8X4),
-                    lhsT_scale=sc[:, c0 : c0 + P],
-                    rhs=w_cod[:, 256 * k : 256 * k + 256].bitcast(FP8X4),
-                    rhs_scale=w_scl[:, 256 * k : 256 * k + 256],
-                    start=(k == 0),
-                    stop=(k == KC - 1),
-                )
+        def mx(b, h):
+            if b < B - 2:
+                zp = ps_z.tile([P, 512], F32, name="zp", tag="zp")
+            else:
+                zp = ps_t.tile([P, 512], F32, name="zp", tag="tp")
+            zp_of[(b, h)] = zp
+            for a in range(2):
+                for k in range(KC):
+                    c0 = P * (NT * k + 2 * h + a)
+                    nc.tensor.matmul_mx(
+                        out=zp[:, 256 * a : 256 * a + 256],
+                        lhsT=cd_of[b][:, c0 : c0 + P].bitcast(FP8X4),
+                        lhsT_scale=sc_of[b][:, c0 : c0 + P],
+                        rhs=w_cod[:, 256 * k : 256 * k + 256].bitcast(FP8X4),
+                        rhs_scale=w_scl[:, 256 * k : 256 * k + 256],
+                        start=(k == 0),
+                        stop=(k == KC - 1),
+                    )
 
         def weigh(b, h):
             if h == 0:
@@ -263,13 +259,14 @@ def tile_dygcn_pb_t_kernel(tc, x_g, emb, weights_pool, bias_pool, out):
                 bias_product_turn()
             if i == 7:
                 bias_product_multiply()
-            for third in range(3):
+            for h in range(2):
                 if i < B:
-                    transpose_bank(i, 2 * third)
-                    transpose_bank(i, 2 * third + 1)
-                    order_words(i + 1, 4 * third + 2, ORD_UNITS[third])
+                    for j in range(3 * h, 3 * h + 3):
+                        transpose_bank(i, j)
+                    for u0 in ((2,), (8,))[h] if i >= 4 else ((), (2, 8))[h]:
+                        order_words(i + 1, u0, 2, 1, nc.scalar.copy)
                 if 2 <= i < B + 2:
-                    mx_third(i - 2, third)
+                    mx(i - 2, h)
             if i == 0:
                 quantise(0, 0, 512)
                 quantise(0, 512, 512)
@@ -301,9 +298,13 @@ def tile_dygcn_pb_t_kernel(tc, x_g, emb, weights_pool, bias_pool, out):
                     finish(b - 1, 2, rs_of[b // 2][:], nc.gpsimd, nc.sync)
                 if b == 3:
                     finish(0, 2, rs_of[0][:], nc.gpsimd, nc.sync)
+            if i >= 4:
+                order_words(i + 1, 5, 2, 6, nc.vector.tensor_copy)
             if 2 <= i < B:
                 quantise(i - 1, 0, 1024)
                 quantise(i - 1, 1024, 512)
+            if i < 4:
+                order_words(i + 1, 5, 2, 6, nc.vector.tensor_copy)
         finish(B - 2, 1, sum_on_gpsimd(B - 2), nc.gpsimd, nc.sync)
         reduce(B - 1)
         finish(B - 1, 1, rs_of[B // 2 - 1][:, BO:], nc.vector, nc.scalar)

@@ -33,7 +33,7 @@ def tile_dygcn_pb_t_kernel(tc, x_g, emb, weights_pool, bias_pool, out):
         gpool = ctx.enter_context(tc.tile_pool(name="gpool", bufs=3))
         cpool = ctx.enter_context(tc.tile_pool(name="cpool", bufs=3))
         ppool = ctx.enter_context(tc.tile_pool(name="ppool", bufs=4))
-        qpool = ctx.enter_context(tc.tile_pool(name="qpool", bufs=7))
+        qpool = ctx.enter_context(tc.tile_pool(name="qpool", bufs=4))
         opool = ctx.enter_context(tc.tile_pool(name="opool", bufs=2))
         ps_t = ctx.enter_context(tc.psum_pool(name="ps_t", bufs=6))
         ps_z = ctx.enter_context(tc.psum_pool(name="ps_z", bufs=2))
@@ -168,7 +168,7 @@ def tile_dygcn_pb_t_kernel(tc, x_g, emb, weights_pool, bias_pool, out):
 
         def weigh_and_fold(b, h):
             weigh(b, h)
-            if B - 3 <= b < B - 1:
+            if b < B - 1:
                 fold_16_to_8(b, h)
 
         def reduce(b):

from contextlib import ExitStack

import concourse.mybir as mybir
from concourse.masks import make_identity

BF16 = mybir.dt.bfloat16
F32 = mybir.dt.float32
U32 = mybir.dt.uint32
U8 = mybir.dt.uint8
FP8X4 = mybir.dt.float8_e4m3fn_x4
ADD = mybir.AluOpType.add
MULT = mybir.AluOpType.mult
AX = mybir.AxisListType.X

P = 128
B, KC, N, F, O, E = 16, 3, 512, 512, 16, 16
NT = N // P
UNITS = KC * NT
NB = 6
BO = NT * O
SPLIT = 3
EMB_FIRST = 4
ORD_FIRST = 4

FLOPS = 2 * B * N * KC * F * E * O + 4 * B * N * E * O


def tile_dygcn_pb_t_kernel(tc, x_g, emb, weights_pool, bias_pool, out):
    nc = tc.nc
    with ExitStack() as ctx:
        const = ctx.enter_context(tc.tile_pool(name="const", bufs=1))
        xpool = ctx.enter_context(tc.tile_pool(name="xpool", bufs=NB))
        gpool = ctx.enter_context(tc.tile_pool(name="gpool", bufs=3))
        cpool = ctx.enter_context(tc.tile_pool(name="cpool", bufs=3))
        ppool = ctx.enter_context(tc.tile_pool(name="ppool", bufs=4))
        qpool = ctx.enter_context(tc.tile_pool(name="qpool", bufs=4))
        opool = ctx.enter_context(tc.tile_pool(name="opool", bufs=2))
        ps_t = ctx.enter_context(tc.psum_pool(name="ps_t", bufs=6))
        ps_z = ctx.enter_context(tc.psum_pool(name="ps_z", bufs=2))
        ctx.enter_context(tc.manual_schedule())

        ident_f = const.tile([P, P], F32, name="ident_f")
        ident_b = const.tile([P, P], BF16, name="ident_b")
        w_raw = const.tile([P, KC * E * 4 * O], BF16, name="w_raw")
        w_grp = const.tile([P, KC * 512], F32, name="w_grp", align_bytes=64)
        w_cod = const.tile([P, KC * 256], U32, name="w_cod", align_bytes=64)
        w_scl = const.tile([P, KC * 256], U8, name="w_scl", align_bytes=64)
        g_bf = const.tile([P, B * NT * E], BF16, name="g_bf")
        g_32 = const.tile([P, B * NT, E], F32, name="g_32")
        g_t = const.tile([P, B * NT * E], BF16, name="g_t")
        bdiag = const.tile([P, P], BF16, name="bdiag")
        gb = const.tile([P, B * BO], F32, name="gb")
        o_sb = const.tile([P, B * BO], F32, name="o_sb")

        xs_of = {}
        xo_of = {}
        gr_of = {}
        cd_of = {}
        sc_of = {}
        zp_of = {}
        pr_of = {}
        q1_of = {}
        rs_of = {}

        def load_x(b, split):
            xs = xpool.tile([P, KC * NT * F], BF16, name="xs")
            xs_of[b] = xs
            src = x_g[b].rearrange("k (p t) f -> p k (t f)", t=NT)
            dst = xs[:].rearrange("p (k c) -> p k c", k=KC)
            if split:
                for k in range(KC):
                    nc.sync.dma_start(out=dst[:, k, :], in_=src[:, k, :])
            else:
                nc.sync.dma_start(out=dst, in_=src)

        def load_emb(b0, b1):
            nc.sync.dma_start(
                out=g_bf[:].rearrange("p (b c) -> p b c", b=B)[:, b0:b1],
                in_=emb.rearrange("b (p t) e -> p b (t e)", t=NT)[:, b0:b1],
            )

        def emb_to_float32(b0, b1):
            nc.vector.tensor_copy(
                out=g_32[:, NT * b0 : NT * b1, :].rearrange("p t e -> p (t e)"),
                in_=g_bf[:, NT * E * b0 : NT * E * b1],
            )

        def new_batch(b):
            gr_of[b] = gpool.tile([P, UNITS * 256], F32, name="gr", align_bytes=64)
            cd_of[b] = cpool.tile([P, UNITS * P], U32, name="cd", align_bytes=64)
            sc_of[b] = cpool.tile([P, UNITS * P], U8, name="sc", align_bytes=64)

        def order_words(b, u0, units, step, copy):
            if not ORD_FIRST <= b < B:
                return
            xo = opool.tile([P, units, 256], F32, name="xo%d" % u0)
            for d in range(units):
                xo_of[(b, u0 + step * d)] = xo[:, d, :]
            copy(
                out=xo[:].rearrange("p a (u m) -> p a u m", u=2),
                in_=xs_of[b][:]
                .bitcast(F32)
                .rearrange("p (c w) -> p c w", w=256)[:, u0 : u0 + step * (units - 1) + 1 : step]
                .rearrange("p a (m u) -> p a u m", u=2),
            )

        def transpose_bank(b, j):
            xw = xs_of[b][:].bitcast(F32)
            tp = ps_t.tile([P, 512], F32, name="tp", tag="tp")
            for s in range(4):
                unit, half = 2 * j + s // 2, s % 2
                words = xw[:, 256 * unit + half : 256 * unit + 256 : 2]
                if (b, unit) in xo_of:
                    words = xo_of[(b, unit)][:, P * half : P * half + P]
                nc.tensor.transpose(tp[:, P * s : P * s + P], words, ident_f[:])
            nc.scalar.copy(
                out=gr_of[b][:, 512 * j : 512 * j + 512].rearrange("p (a n u) -> p a n u", a=2, u=2),
                in_=tp[:].rearrange("p (a u n) -> p a n u", a=2, u=2),
            )

        def quantise(b, c0, cw):
            nc.vector.quantize_mx(
                out=cd_of[b][:, c0 : c0 + cw].bitcast(FP8X4),
                scales=sc_of[b][:, c0 : c0 + cw],
                in_=gr_of[b][:, 2 * c0 : 2 * (c0 + cw)].bitcast(BF16),
            )

        def mx(b, h):
            if b < B - 2:
                zp = ps_z.tile([P, 512], F32, name="zp", tag="zp")
            else:
                zp = ps_t.tile([P, 512], F32, name="zp", tag="tp")
            zp_of[(b, h)] = zp
            for a in range(2):
                for k in range(KC):
                    c0 = P * (NT * k + 2 * h + a)
                    nc.tensor.matmul_mx(
                        out=zp[:, 256 * a : 256 * a + 256],
                        lhsT=cd_of[b][:, c0 : c0 + P].bitcast(FP8X4),
                        lhsT_scale=sc_of[b][:, c0 : c0 + P],
                        rhs=w_cod[:, 256 * k : 256 * k + 256].bitcast(FP8X4),
                        rhs_scale=w_scl[:, 256 * k : 256 * k + 256],
                        start=(k == 0),
                        stop=(k == KC - 1),
                    )

        def weigh(b, h):
            if h == 0:
                pr_of[b] = ppool.tile([P, NT * O * E], F32, name="pr")
            t0 = NT * b + 2 * h
            nc.vector.tensor_tensor(
                out=pr_of[b][:, 512 * h : 512 * h + 512].rearrange("p (a o e) -> p a o e", a=2, o=O),
                in0=zp_of[(b, h)][:].rearrange("p (a o e) -> p a o e", a=2, o=O),
                in1=g_32[:, t0 : t0 + 2, :].unsqueeze(2).to_broadcast([P, 2, O, E]),
                op=MULT,
            )

        def fold_16_to_8(b, h):
            if h == 0:
                q1_of[b] = qpool.tile([P, BO * 8], F32, name="q1")
            pv = pr_of[b][:, 512 * h : 512 * h + 512].rearrange("p (c e) -> p c e", e=E)
            nc.gpsimd.tensor_tensor(
                out=q1_of[b][:, 256 * h : 256 * h + 256].rearrange("p (c e) -> p c e", e=8),
                in0=pv[:, :, 0:8],
                in1=pv[:, :, 8:16],
                op=ADD,
            )

        def weigh_and_fold(b, h):
            weigh(b, h)
            if b < B - 1:
                fold_16_to_8(b, h)

        def reduce(b):
            terms, width = (q1_of[b], 8) if b in q1_of else (pr_of[b], E)
            if b // 2 not in rs_of:
                rs_of[b // 2] = ppool.tile([P, 2 * BO], F32, name="rs")
            c0 = BO * (b % 2)
            nc.vector.tensor_reduce(
                out=rs_of[b // 2][:, c0 : c0 + BO],
                in_=terms[:].rearrange("p (c e) -> p c e", e=width),
                axis=AX,
                op=ADD,
            )

        def finish(b0, count, sums, adder, queue):
            cols = slice(BO * b0, BO * (b0 + count))
            adder.tensor_tensor(out=o_sb[:, cols], in0=sums, in1=gb[:, cols], op=ADD)
            queue.dma_start(
                out=out[b0 : b0 + count].rearrange("b (p t) o -> p b (t o)", t=NT),
                in_=o_sb[:, cols].rearrange("p (b c) -> p b c", b=count),
            )

        def sum_on_gpsimd(b):
            terms, width = q1_of[b][:], 8
            while width > 1:
                half = width // 2
                tv = terms.rearrange("p (c e) -> p c e", e=width)
                nxt = ppool.tile([P, BO * half], F32, name="fold%d" % half)
                nc.gpsimd.tensor_tensor(
                    out=nxt[:].rearrange("p (c e) -> p c e", e=half),
                    in0=tv[:, :, 0:half],
                    in1=tv[:, :, half:width],
                    op=ADD,
                )
                terms, width = nxt[:], half
            return terms

        def bias_product_turn():
            tpb = ps_t.tile([P, 1024], BF16, name="tpb", tag="tp")
            for c in range(8):
                nc.tensor.transpose(tpb[:, P * c : P * c + P], g_bf[:, P * c : P * c + P], ident_b[:])
            nc.scalar.copy(out=g_t[:], in_=tpb[:])

        def bias_product_multiply():
            for half in range(2):
                gp = ps_t.tile([P, 512], F32, name="gp", tag="tp")
                for c4 in range(4):
                    c = 4 * half + c4
                    nc.tensor.matmul(
                        gp[:, P * c4 : P * c4 + P],
                        lhsT=g_t[:, P * c : P * c + P],
                        rhs=bdiag[:],
                        start=True,
                        stop=True,
                    )
                nc.scalar.copy(out=gb[:, 512 * half : 512 * half + 512], in_=gp[:])

        make_identity(nc, ident_f[:])
        make_identity(nc, ident_b[:])
        nc.vector.memset(bdiag[:], 0.0)
        for i in range(8):
            nc.gpsimd.dma_start(out=bdiag[16 * i : 16 * i + 16, 16 * i : 16 * i + 16], in_=bias_pool)

        load_x(0, True)
        for k in range(KC):
            nc.sync.dma_start(
                out=w_raw[:].rearrange("p (k e c) -> p k e c", k=KC, e=E)[:, k],
                in_=weights_pool.rearrange("e k (p t) o -> p k e (t o)", t=4)[:, k],
            )
        for b in range(1, NB):
            load_x(b, b <= SPLIT)
            if b == 1:
                load_emb(0, EMB_FIRST)
        load_emb(EMB_FIRST, B)

        def w_turn(k, copy):
            copy(
                out=w_grp[:, 512 * k : 512 * k + 512].bitcast(BF16).rearrange("p (o e t) -> p o e t", o=O, e=E),
                in_=w_raw[:, 1024 * k : 1024 * k + 1024].rearrange("p (e t o) -> p o e t", e=E, t=4),
            )

        for i in range(B + 3):
            if i < B:
                if i > 0 and i + NB - 1 < B:
                    load_x(i + NB - 1, False)
                new_batch(i)
            if i == 6:
                bias_product_turn()
            if i == 7:
                bias_product_multiply()
            for h in range(2):
                if i < B:
                    for j in range(3 * h, 3 * h + 3):
                        transpose_bank(i, j)
                    for u0 in ((2,), (8,))[h] if i >= 4 else ((), (2, 8))[h]:
                        order_words(i + 1, u0, 2, 1, nc.scalar.copy)
                if 2 <= i < B + 2:
                    mx(i - 2, h)
            if i == 0:
                quantise(0, 0, 512)
                quantise(0, 512, 512)
                quantise(0, 1024, 512)
                w_turn(0, nc.vector.tensor_copy)
                w_turn(1, nc.scalar.copy)
                w_turn(2, nc.vector.tensor_copy)
                for c0, c1 in ((0, 512), (512, 768)):
                    nc.vector.quantize_mx(
                        out=w_cod[:, c0:c1].bitcast(FP8X4),
                        scales=w_scl[:, c0:c1],
                        in_=w_grp[:, 2 * c0 : 2 * c1].bitcast(BF16),
                    )
            if i == 2:
                emb_to_float32(0, EMB_FIRST)
            if i >= 3:
                weigh_and_fold(i - 3, 0)
                if i == B:
                    reduce(B - 4)
                    quantise(B - 1, 0, 1024)
                    quantise(B - 1, 1024, 512)
                weigh_and_fold(i - 3, 1)
            if i == 6:
                emb_to_float32(EMB_FIRST, B)
            if 4 <= i < B or i == B + 1:
                b = i - 4
                reduce(b)
                if b >= 3 and b % 2 == 1:
                    finish(b - 1, 2, rs_of[b // 2][:], nc.gpsimd, nc.sync)
                if b == 3:
                    finish(0, 2, rs_of[0][:], nc.gpsimd, nc.sync)
            if i >= 4:
                order_words(i + 1, 5, 2, 6, nc.vector.tensor_copy)
            if 2 <= i < B:
                quantise(i - 1, 0, 1024)
                quantise(i - 1, 1024, 512)
            if i < 4:
                order_words(i + 1, 5, 2, 6, nc.vector.tensor_copy)
        finish(B - 2, 1, sum_on_gpsimd(B - 2), nc.gpsimd, nc.sync)
        reduce(B - 1)
        finish(B - 1, 1, rs_of[B // 2 - 1][:, BO:], nc.vector, nc.scalar)
